import numpy as np
import ml_dtypes

BF16 = ml_dtypes.bfloat16


def bf(x):
    return np.asarray(x, np.float32).astype(BF16)


def f32(x):
    return np.asarray(x, np.float32)


def f64(x):
    return np.asarray(x).astype(np.float64)


def striped(idx):
    return np.tile(idx.reshape(-1, 16).T, (8, 1))


C, S, N = 256, 1024, 2048


def setup_inputs():
    return {"weights": f32(0.25 * np.random.standard_normal((C, S))), "patches": f32(np.random.standard_normal((C, N))), "offs": striped(np.random.permutation(np.tile(np.arange(S), 2))[:N])}


def reference(weights, patches, offs):
    idx = offs[:16].T.reshape(-1)
    return (f64(weights)[:, idx] * f64(patches)).sum(axis=0, keepdims=True)

@@ -1,0 +1,56 @@
+import concourse.mybir as mybir
+
+F32, BF16, U16 = mybir.dt.float32, mybir.dt.bfloat16, mybir.dt.uint16
+
+P = 128
+C, S, N = 256, 1024, 2048
+BLOCKS = C // P
+PIECE = 512
+PIECES = N // PIECE
+
+FLOPS = 2 * C * N
+
+
+def tile_kernellookup_kernel(tc, weights, patches, offs, out):
+    nc = tc.nc
+    mult = mybir.AluOpType.mult
+    copy = mybir.ActivationFunctionType.Copy
+
+    with (
+        tc.tile_pool(name="held", bufs=1) as held,
+        tc.tile_pool(name="work", bufs=4) as work,
+        tc.psum_pool(name="sums", bufs=1) as sums,
+    ):
+        offsets = held.tile([P, N // 16], U16, name="offsets")
+        nc.sync.dma_start(offsets[:], offs)
+
+        bank = []
+        patch = []
+        for b in range(BLOCKS):
+            rows = slice(b * P, (b + 1) * P)
+            bank.append(held.tile([P, S], F32, name=f"bank{b}"))
+            nc.sync.dma_start(bank[b][:], weights[rows, :])
+            patch.append([])
+            for k in range(PIECES):
+                patch[b].append(held.tile([P, PIECE], F32, name=f"patch{b}_{k}"))
+                nc.sync.dma_start(patch[b][k][:], patches[rows, k * PIECE : (k + 1) * PIECE])
+
+        ones = held.tile([P, 1], BF16, name="ones")
+        nc.vector.memset(ones[:], 1.0)
+
+        total = [sums.tile([1, PIECE], F32, name=f"total{k}") for k in range(PIECES)]
+        result = held.tile([1, N], F32, name="result")
+
+        for b in range(BLOCKS):
+            for k in range(PIECES):
+                picked = bank[b][:].indirect(offsets[:, k * (PIECE // 16) : (k + 1) * (PIECE // 16)])
+                product = work.tile([P, PIECE], F32, name="product")
+                nc.vector.tensor_tensor(product[:], picked, patch[b][k][:], mult)
+                rounded = work.tile([P, PIECE], BF16, name="rounded")
+                nc.scalar.activation(rounded[:], product[:], copy)
+                nc.tensor.matmul(total[k][:], ones[:], rounded[:], start=(b == 0), stop=(b == BLOCKS - 1))
+
+        for k in range(PIECES):
+            pixels = slice(k * PIECE, (k + 1) * PIECE)
+            nc.scalar.activation(result[:, pixels], total[k][:], copy)
+            nc.sync.dma_start(out[:, pixels], result[:, pixels])

@@ -7,6 +7,8 @@ C, S, N = 256, 1024, 2048
 BLOCKS = C // P
 PIECE = 512
 PIECES = N // PIECE
+ROW = 128
+ROWS = N // ROW
 
 FLOPS = 2 * C * N
 
@@ -35,11 +37,11 @@ def tile_kernellookup_kernel(tc, weights, patches, offs, out):
                 patch[b].append(held.tile([P, PIECE], F32, name=f"patch{b}_{k}"))
                 nc.sync.dma_start(patch[b][k][:], patches[rows, k * PIECE : (k + 1) * PIECE])
 
-        ones = held.tile([P, 1], BF16, name="ones")
-        nc.vector.memset(ones[:], 1.0)
+        slide = held.tile([P, 2 * ROWS - 1], BF16, name="slide")
+        nc.vector.memset(slide[:], 0.0)
+        nc.vector.memset(slide[:, ROWS - 1 : ROWS], 1.0)
 
-        total = [sums.tile([1, PIECE], F32, name=f"total{k}") for k in range(PIECES)]
-        result = held.tile([1, N], F32, name="result")
+        total = sums.tile([ROWS, ROW], F32, name="total")
 
         for b in range(BLOCKS):
             for k in range(PIECES):
@@ -48,9 +50,16 @@ def tile_kernellookup_kernel(tc, weights, patches, offs, out):
                 nc.vector.tensor_tensor(product[:], picked, patch[b][k][:], mult)
                 rounded = work.tile([P, PIECE], BF16, name="rounded")
                 nc.scalar.activation(rounded[:], product[:], copy)
-                nc.tensor.matmul(total[k][:], ones[:], rounded[:], start=(b == 0), stop=(b == BLOCKS - 1))
+                for i in range(PIECE // ROW):
+                    r = k * (PIECE // ROW) + i
+                    nc.tensor.matmul(
+                        total[:],
+                        slide[:, ROWS - 1 - r : 2 * ROWS - 1 - r],
+                        rounded[:, i * ROW : (i + 1) * ROW],
+                        start=(b == 0 and r == 0),
+                        stop=(b == BLOCKS - 1 and r == ROWS - 1),
+                    )
 
-        for k in range(PIECES):
-            pixels = slice(k * PIECE, (k + 1) * PIECE)
-            nc.scalar.activation(result[:, pixels], total[k][:], copy)
-            nc.sync.dma_start(out[:, pixels], result[:, pixels])
+        result = held.tile([ROWS, ROW], F32, name="result")
+        nc.scalar.activation(result[:], total[:], copy)
+        nc.sync.dma_start(out.rearrange("o (r c) -> (o r) c", c=ROW), result[:])

@@ -5,7 +5,7 @@ F32, BF16, U16 = mybir.dt.float32, mybir.dt.bfloat16, mybir.dt.uint16
 P = 128
 C, S, N = 256, 1024, 2048
 BLOCKS = C // P
-PIECE = 512
+PIECE = 256
 PIECES = N // PIECE
 ROW = 128
 ROWS = N // ROW

@@ -5,12 +5,17 @@ F32, BF16, U16 = mybir.dt.float32, mybir.dt.bfloat16, mybir.dt.uint16
 P = 128
 C, S, N = 256, 1024, 2048
 BLOCKS = C // P
-PIECE = 256
-PIECES = N // PIECE
 ROW = 128
 ROWS = N // ROW
+GROWING = (128, 128, 256, 512, 512, 512)
+WIDTHS = (GROWING, tuple(reversed(GROWING)))
+assert len(WIDTHS) == BLOCKS and sum(GROWING) == N and all(width % ROW == 0 for width in GROWING)
 
 FLOPS = 2 * C * N
+
+
+def cut(widths):
+    return [(sum(widths[:k]), width) for k, width in enumerate(widths)]
 
 
 def tile_kernellookup_kernel(tc, weights, patches, offs, out):
@@ -33,9 +38,9 @@ def tile_kernellookup_kernel(tc, weights, patches, offs, out):
             bank.append(held.tile([P, S], F32, name=f"bank{b}"))
             nc.sync.dma_start(bank[b][:], weights[rows, :])
             patch.append([])
-            for k in range(PIECES):
-                patch[b].append(held.tile([P, PIECE], F32, name=f"patch{b}_{k}"))
-                nc.sync.dma_start(patch[b][k][:], patches[rows, k * PIECE : (k + 1) * PIECE])
+            for k, (first, width) in enumerate(cut(WIDTHS[b])):
+                patch[b].append(held.tile([P, width], F32, name=f"patch{b}_{k}"))
+                nc.sync.dma_start(patch[b][k][:], patches[rows, first : first + width])
 
         slide = held.tile([P, 2 * ROWS - 1], BF16, name="slide")
         nc.vector.memset(slide[:], 0.0)
@@ -44,14 +49,14 @@ def tile_kernellookup_kernel(tc, weights, patches, offs, out):
         total = sums.tile([ROWS, ROW], F32, name="total")
 
         for b in range(BLOCKS):
-            for k in range(PIECES):
-                picked = bank[b][:].indirect(offsets[:, k * (PIECE // 16) : (k + 1) * (PIECE // 16)])
-                product = work.tile([P, PIECE], F32, name="product")
+            for k, (first, width) in enumerate(cut(WIDTHS[b])):
+                picked = bank[b][:].indirect(offsets[:, first // 16 : (first + width) // 16])
+                product = work.tile([P, width], F32, name="product")
                 nc.vector.tensor_tensor(product[:], picked, patch[b][k][:], mult)
-                rounded = work.tile([P, PIECE], BF16, name="rounded")
+                rounded = work.tile([P, width], BF16, name="rounded")
                 nc.scalar.activation(rounded[:], product[:], copy)
-                for i in range(PIECE // ROW):
-                    r = k * (PIECE // ROW) + i
+                for i in range(width // ROW):
+                    r = first // ROW + i
                     nc.tensor.matmul(
                         total[:],
                         slide[:, ROWS - 1 - r : 2 * ROWS - 1 - r],

@@ -54,7 +54,10 @@ def tile_kernellookup_kernel(tc, weights, patches, offs, out):
                 product = work.tile([P, width], F32, name="product")
                 nc.vector.tensor_tensor(product[:], picked, patch[b][k][:], mult)
                 rounded = work.tile([P, width], BF16, name="rounded")
-                nc.scalar.activation(rounded[:], product[:], copy)
+                if b == BLOCKS - 1 and first + width == N:
+                    nc.vector.tensor_copy(rounded[:], product[:])
+                else:
+                    nc.scalar.activation(rounded[:], product[:], copy)
                 for i in range(width // ROW):
                     r = first // ROW + i
                     nc.tensor.matmul(

@@ -54,10 +54,7 @@ def tile_kernellookup_kernel(tc, weights, patches, offs, out):
                 product = work.tile([P, width], F32, name="product")
                 nc.vector.tensor_tensor(product[:], picked, patch[b][k][:], mult)
                 rounded = work.tile([P, width], BF16, name="rounded")
-                if b == BLOCKS - 1 and first + width == N:
-                    nc.vector.tensor_copy(rounded[:], product[:])
-                else:
-                    nc.scalar.activation(rounded[:], product[:], copy)
+                nc.scalar.activation(rounded[:], product[:], copy)
                 for i in range(width // ROW):
                     r = first // ROW + i
                     nc.tensor.matmul(
@@ -70,4 +67,4 @@ def tile_kernellookup_kernel(tc, weights, patches, offs, out):
 
         result = held.tile([ROWS, ROW], F32, name="result")
         nc.scalar.activation(result[:], total[:], copy)
-        nc.sync.dma_start(out.rearrange("o (r c) -> (o r) c", c=ROW), result[:])
+        nc.scalar.dma_start(out.rearrange("o (r c) -> (o r) c", c=ROW), result[:])

@@ -54,7 +54,10 @@ def tile_kernellookup_kernel(tc, weights, patches, offs, out):
                 product = work.tile([P, width], F32, name="product")
                 nc.vector.tensor_tensor(product[:], picked, patch[b][k][:], mult)
                 rounded = work.tile([P, width], BF16, name="rounded")
-                nc.scalar.activation(rounded[:], product[:], copy)
+                if b == BLOCKS - 1 and first + width == N:
+                    nc.vector.tensor_copy(rounded[:], product[:])
+                else:
+                    nc.scalar.activation(rounded[:], product[:], copy)
                 for i in range(width // ROW):
                     r = first // ROW + i
                     nc.tensor.matmul(

@@ -25,7 +25,6 @@ def tile_kernellookup_kernel(tc, weights, patches, offs, out):
 
     with (
         tc.tile_pool(name="held", bufs=1) as held,
-        tc.tile_pool(name="work", bufs=4) as work,
         tc.psum_pool(name="sums", bufs=1) as sums,
     ):
         offsets = held.tile([P, N // 16], U16, name="offsets")
@@ -51,9 +50,9 @@ def tile_kernellookup_kernel(tc, weights, patches, offs, out):
         for b in range(BLOCKS):
             for k, (first, width) in enumerate(cut(WIDTHS[b])):
                 picked = bank[b][:].indirect(offsets[:, first // 16 : (first + width) // 16])
-                product = work.tile([P, width], F32, name="product")
+                product = held.tile([P, width], F32, name=f"product{b}_{k}")
                 nc.vector.tensor_tensor(product[:], picked, patch[b][k][:], mult)
-                rounded = work.tile([P, width], BF16, name="rounded")
+                rounded = held.tile([P, width], BF16, name=f"rounded{b}_{k}")
                 if b == BLOCKS - 1 and first + width == N:
                     nc.vector.tensor_copy(rounded[:], product[:])
                 else:

@@ -7,9 +7,10 @@ C, S, N = 256, 1024, 2048
 BLOCKS = C // P
 ROW = 128
 ROWS = N // ROW
-GROWING = (128, 128, 256, 512, 512, 512)
-WIDTHS = (GROWING, tuple(reversed(GROWING)))
-assert len(WIDTHS) == BLOCKS and sum(GROWING) == N and all(width % ROW == 0 for width in GROWING)
+WIDTHS = ((128, 128, 256, 640, 896), (512, 768, 384, 256, 128))
+assert len(WIDTHS) == BLOCKS
+assert all(sum(widths) == N and all(width % ROW == 0 for width in widths) for widths in WIDTHS)
+LOADS_OF_WIDEST = 2
 
 FLOPS = 2 * C * N
 
@@ -39,7 +40,9 @@ def tile_kernellookup_kernel(tc, weights, patches, offs, out):
             patch.append([])
             for k, (first, width) in enumerate(cut(WIDTHS[b])):
                 patch[b].append(held.tile([P, width], F32, name=f"patch{b}_{k}"))
-                nc.sync.dma_start(patch[b][k][:], patches[rows, first : first + width])
+                step = width // LOADS_OF_WIDEST if width == max(WIDTHS[b]) else width
+                for at in range(0, width, step):
+                    nc.sync.dma_start(patch[b][k][:, at : at + step], patches[rows, first + at : first + at + step])
 
         slide = held.tile([P, 2 * ROWS - 1], BF16, name="slide")
         nc.vector.memset(slide[:], 0.0)

@@ -29,7 +29,6 @@ def tile_kernellookup_kernel(tc, weights, patches, offs, out):
         tc.psum_pool(name="sums", bufs=1) as sums,
     ):
         offsets = held.tile([P, N // 16], U16, name="offsets")
-        nc.sync.dma_start(offsets[:], offs)
 
         bank = []
         patch = []
@@ -37,6 +36,8 @@ def tile_kernellookup_kernel(tc, weights, patches, offs, out):
             rows = slice(b * P, (b + 1) * P)
             bank.append(held.tile([P, S], F32, name=f"bank{b}"))
             nc.sync.dma_start(bank[b][:], weights[rows, :])
+            if b == 0:
+                nc.sync.dma_start(offsets[:], offs)
             patch.append([])
             for k, (first, width) in enumerate(cut(WIDTHS[b])):
                 patch[b].append(held.tile([P, width], F32, name=f"patch{b}_{k}"))

@@ -7,10 +7,10 @@ C, S, N = 256, 1024, 2048
 BLOCKS = C // P
 ROW = 128
 ROWS = N // ROW
-WIDTHS = ((128, 128, 256, 640, 896), (512, 768, 384, 256, 128))
+WIDTHS = ((128, 128, 256, 512, 1024), (512, 768, 384, 256, 128))
 assert len(WIDTHS) == BLOCKS
 assert all(sum(widths) == N and all(width % ROW == 0 for width in widths) for widths in WIDTHS)
-LOADS_OF_WIDEST = 2
+LOADS_OF_WIDEST = (1, 3)
 
 FLOPS = 2 * C * N
 
@@ -41,7 +41,7 @@ def tile_kernellookup_kernel(tc, weights, patches, offs, out):
             patch.append([])
             for k, (first, width) in enumerate(cut(WIDTHS[b])):
                 patch[b].append(held.tile([P, width], F32, name=f"patch{b}_{k}"))
-                step = width // LOADS_OF_WIDEST if width == max(WIDTHS[b]) else width
+                step = width // LOADS_OF_WIDEST[b] if width == max(WIDTHS[b]) else width
                 for at in range(0, width, step):
                     nc.sync.dma_start(patch[b][k][:, at : at + step], patches[rows, first + at : first + at + step])
 

@@ -22,7 +22,6 @@ def cut(widths):
 def tile_kernellookup_kernel(tc, weights, patches, offs, out):
     nc = tc.nc
     mult = mybir.AluOpType.mult
-    copy = mybir.ActivationFunctionType.Copy
 
     with (
         tc.tile_pool(name="held", bufs=1) as held,
@@ -60,7 +59,7 @@ def tile_kernellookup_kernel(tc, weights, patches, offs, out):
                 if b == BLOCKS - 1 and first + width == N:
                     nc.vector.tensor_copy(rounded[:], product[:])
                 else:
-                    nc.scalar.activation(rounded[:], product[:], copy)
+                    nc.scalar.copy(rounded[:], product[:])
                 for i in range(width // ROW):
                     r = first // ROW + i
                     nc.tensor.matmul(
@@ -72,5 +71,5 @@ def tile_kernellookup_kernel(tc, weights, patches, offs, out):
                     )
 
         result = held.tile([ROWS, ROW], F32, name="result")
-        nc.scalar.activation(result[:], total[:], copy)
+        nc.scalar.copy(result[:], total[:])
         nc.scalar.dma_start(out.rearrange("o (r c) -> (o r) c", c=ROW), result[:])

import concourse.mybir as mybir

F32, BF16, U16 = mybir.dt.float32, mybir.dt.bfloat16, mybir.dt.uint16

P = 128
C, S, N = 256, 1024, 2048
BLOCKS = C // P
ROW = 128
ROWS = N // ROW
WIDTHS = ((128, 128, 256, 512, 1024), (512, 768, 384, 256, 128))
assert len(WIDTHS) == BLOCKS
assert all(sum(widths) == N and all(width % ROW == 0 for width in widths) for widths in WIDTHS)
LOADS_OF_WIDEST = (1, 3)

FLOPS = 2 * C * N


def cut(widths):
    return [(sum(widths[:k]), width) for k, width in enumerate(widths)]


def tile_kernellookup_kernel(tc, weights, patches, offs, out):
    nc = tc.nc
    mult = mybir.AluOpType.mult

    with (
        tc.tile_pool(name="held", bufs=1) as held,
        tc.psum_pool(name="sums", bufs=1) as sums,
    ):
        offsets = held.tile([P, N // 16], U16, name="offsets")

        bank = []
        patch = []
        for b in range(BLOCKS):
            rows = slice(b * P, (b + 1) * P)
            bank.append(held.tile([P, S], F32, name=f"bank{b}"))
            nc.sync.dma_start(bank[b][:], weights[rows, :])
            if b == 0:
                nc.sync.dma_start(offsets[:], offs)
            patch.append([])
            for k, (first, width) in enumerate(cut(WIDTHS[b])):
                patch[b].append(held.tile([P, width], F32, name=f"patch{b}_{k}"))
                step = width // LOADS_OF_WIDEST[b] if width == max(WIDTHS[b]) else width
                for at in range(0, width, step):
                    nc.sync.dma_start(patch[b][k][:, at : at + step], patches[rows, first + at : first + at + step])

        slide = held.tile([P, 2 * ROWS - 1], BF16, name="slide")
        nc.vector.memset(slide[:], 0.0)
        nc.vector.memset(slide[:, ROWS - 1 : ROWS], 1.0)

        total = sums.tile([ROWS, ROW], F32, name="total")

        for b in range(BLOCKS):
            for k, (first, width) in enumerate(cut(WIDTHS[b])):
                picked = bank[b][:].indirect(offsets[:, first // 16 : (first + width) // 16])
                product = held.tile([P, width], F32, name=f"product{b}_{k}")
                nc.vector.tensor_tensor(product[:], picked, patch[b][k][:], mult)
                rounded = held.tile([P, width], BF16, name=f"rounded{b}_{k}")
                if b == BLOCKS - 1 and first + width == N:
                    nc.vector.tensor_copy(rounded[:], product[:])
                else:
                    nc.scalar.copy(rounded[:], product[:])
                for i in range(width // ROW):
                    r = first // ROW + i
                    nc.tensor.matmul(
                        total[:],
                        slide[:, ROWS - 1 - r : 2 * ROWS - 1 - r],
                        rounded[:, i * ROW : (i + 1) * ROW],
                        start=(b == 0 and r == 0),
                        stop=(b == BLOCKS - 1 and r == ROWS - 1),
                    )

        result = held.tile([ROWS, ROW], F32, name="result")
        nc.scalar.copy(result[:], total[:])
        nc.scalar.dma_start(out.rearrange("o (r c) -> (o r) c", c=ROW), result[:])
